import numpy as np
import ml_dtypes


def mxq(x, axis, fmt="e4m3"):
    dtype, down = {"e4m3": (ml_dtypes.float8_e4m3fn, 7), "e5m2": (ml_dtypes.float8_e5m2, 14)}[fmt]
    v = np.moveaxis(np.asarray(x, np.float32).astype(ml_dtypes.bfloat16).astype(np.float64), axis, -1)
    blocks = v.reshape(v.shape[:-1] + (-1, 32))
    amax = np.abs(blocks).max(-1, keepdims=True)
    byte = np.maximum(np.where(amax > 0, np.frexp(amax)[1] - 1 + 127, 0) - down, 1)
    scale = np.exp2(byte - 127.0)
    codes = (blocks / scale).astype(np.float32).astype(dtype).astype(np.float64)
    return np.moveaxis((codes * scale).reshape(v.shape), -1, axis)


WIDE = False


def mx_kscale(k):
    if not WIDE:
        return np.ones(k)
    levels = np.array([10, -10, 5, -5, 0])
    a = np.random.permutation(np.resize(levels, k // 512 * 4)).reshape(k // 512, 4)
    idx = np.arange(k)
    return np.exp2(a[idx // 512, idx % 128 // 32])


BF16 = ml_dtypes.bfloat16


def bf(x):
    return np.asarray(x, np.float32).astype(BF16)


def f64(x):
    return np.asarray(x).astype(np.float64)


B, S, IN, OUT, A, R = 8, 1024, 1024, 128, 8, 128
G = B // A
SCALING = 2.0


def setup_inputs():
    s = mx_kscale(IN)
    return {"data": bf(np.random.standard_normal((B, S, IN)) * s),
            "W": bf(np.random.standard_normal((OUT, IN)) / np.sqrt(IN) / s),
            "t_lora": bf(np.random.standard_normal((A, G, S, R))),
            "lora_b": bf(np.random.standard_normal((A, OUT, R)) * 0.5 / np.sqrt(R))}


def reference(data, W, t_lora, lora_b):
    base = mxq(f64(data), 2, "e4m3") @ mxq(f64(W), 1, "e4m3").T
    delta = (f64(t_lora).reshape(A, G * S, R) @ f64(lora_b).transpose(0, 2, 1)) * SCALING
    return base + delta.reshape(B, S, OUT)

@@ -1,0 +1,161 @@
+from contextlib import ExitStack
+
+import concourse.bass as bass
+import concourse.mybir as mybir
+import concourse.tile as tile
+from concourse.masks import make_identity
+
+F32 = mybir.dt.float32
+BF16 = mybir.dt.bfloat16
+U32 = mybir.dt.uint32
+U8 = mybir.dt.uint8
+FP8X4 = mybir.dt.float8_e4m3fn_x4
+ADD = mybir.AluOpType.add
+
+P = 128
+A = 8
+S = 1024
+K = 1024
+O = 128
+R = 128
+J = 8
+JC = 4
+NCH = A * J // JC
+FLOPS = 2 * A * S * K * O + 2 * A * S * R * O
+
+MANUAL = True
+LAG = 2
+V_BANKS = frozenset(range(3, 64, 8))
+
+
+def tile_linear_pa_t_kernel(tc, data, W, t_lora, lora_b, out):
+    nc = tc.nc
+    with ExitStack() as ctx:
+        if MANUAL:
+            ctx.enter_context(tc.manual_schedule())
+        const = ctx.enter_context(tc.tile_pool(name="const", bufs=1))
+        xpool = ctx.enter_context(tc.tile_pool(name="xpool", bufs=10))
+        opool = ctx.enter_context(tc.tile_pool(name="opool", bufs=1))
+        ttp = ctx.enter_context(tc.tile_pool(name="ttp", bufs=3))
+        gpool = ctx.enter_context(tc.tile_pool(name="gpool", bufs=3))
+        cpool = ctx.enter_context(tc.tile_pool(name="cpool", bufs=3))
+        psum = ctx.enter_context(tc.psum_pool(name="psum", bufs=1))
+
+        data_v = data.rearrange("a (p j) k -> a p j k", j=J)
+        t_v = t_lora.rearrange("a g (p j) r -> p (a g) (j r)", j=J)
+        out_v = out.rearrange("a (p j) o -> a p (j o)", j=J)
+        lb_v = lora_b.rearrange("a o r -> o a r")
+
+        ident_f = const.tile([P, P], F32, name="ident_f")
+        ident_b = const.tile([P, P], BF16, name="ident_b")
+        make_identity(nc, ident_b[:])
+        make_identity(nc, ident_f[:])
+
+        lb_sb = const.tile([P, A, R], BF16, name="lb_sb")
+        nc.sync.dma_start(out=lb_sb[:], in_=lb_v)
+        t_a = const.tile([P, 2, J * R], BF16, name="t_a")
+        nc.sync.dma_start(out=t_a[:], in_=t_v[:, 0:2, :])
+        w_sb = const.tile([P, K], BF16, name="w_sb")
+        nc.sync.dma_start(out=w_sb[:], in_=W)
+        t_b = const.tile([P, A - 2, J * R], BF16, name="t_b")
+        nc.sync.dma_start(out=t_b[:], in_=t_v[:, 2:A, :])
+        x_tiles = []
+        for c in range(NCH):
+            x_sb = xpool.tile([P, JC, K], BF16, name="x_sb")
+            a, h = divmod(c, J // JC)
+            nc.sync.dma_start(out=x_sb[:], in_=data_v[a, :, h * JC:(h + 1) * JC, :])
+            x_tiles.append(x_sb)
+
+        o_tiles = [opool.tile([P, JC * O], F32, name="o_sb%d" % c) for c in range(NCH)]
+
+        def words_out(eng_is_vector, dst_f32, bank):
+            src = bank[:].rearrange("p (g u) t -> p g t u", u=2)
+            dst = dst_f32.rearrange("p (g t u) -> p g t u", g=2, u=2)
+            if eng_is_vector:
+                nc.vector.tensor_copy(out=dst, in_=src)
+            else:
+                nc.scalar.copy(out=dst, in_=src)
+
+        lbT = const.tile([P, A, O], BF16, name="lbT")
+        lbp = psum.tile([P, A, O], BF16, name="lbp", tag="acc", bufs=2)
+        for a in range(A):
+            nc.tensor.transpose(lbp[:, a, :], lb_sb[:, a, :], ident_b[:])
+        nc.vector.tensor_copy(out=lbT[:], in_=lbp[:])
+
+        w_grp = const.tile([P, K], BF16, name="w_grp", align_bytes=64)
+        w_codes = const.tile([P, K // 4], U32, name="w_codes", align_bytes=64)
+        w_scales = const.tile([P, K // 4], U8, name="w_scales", align_bytes=64)
+
+        tT = {}
+        for a in range(A + 1):
+            if a < A:
+                src = t_a[:, a, :] if a < 2 else t_b[:, a - 2, :]
+                tlp = psum.tile([P, J, P], BF16, name="tlp", tag="acc", bufs=2)
+                for j in range(J):
+                    nc.tensor.transpose(tlp[:, j, :], src[:, j * R:(j + 1) * R], ident_b[:])
+                tT[a] = ttp.tile([P, J, P], BF16, name="tT")
+                nc.vector.tensor_copy(out=tT[a][:], in_=tlp[:])
+            if a == 1:
+                wp = psum.tile([P, 4, P], F32, name="wp", tag="xt", bufs=6)
+                w_f = w_sb[:].bitcast(F32)
+                for u in range(4):
+                    nc.tensor.transpose(wp[:, u, :], w_f[:, u * P:(u + 1) * P], ident_f[:])
+                words_out(False, w_grp[:].bitcast(F32), wp)
+            if a == 3:
+                nc.vector.quantize_mx(out=w_codes[:].bitcast(FP8X4), scales=w_scales[:], in_=w_grp[:])
+            if a >= 1:
+                b = a - 1
+                for h in range(J // JC):
+                    dl = psum.tile([P, JC * O], F32, name="dl", tag="xt", bufs=6)
+                    for j in range(JC):
+                        nc.tensor.matmul(dl[:, j * O:(j + 1) * O], lhsT=tT[b][:, h * JC + j, :],
+                                         rhs=lbT[:, b, :], start=True, stop=True)
+                    dst = o_tiles[b * (J // JC) + h]
+                    if h == 1 and b % 2 == 0:
+                        nc.vector.tensor_scalar_mul(out=dst[:], in0=dl[:], scalar1=2.0)
+                    else:
+                        nc.scalar.mul(out=dst[:], in_=dl[:], mul=2.0)
+
+        grp = {}
+        codes = {}
+        scales = {}
+        for s in range(NCH + LAG):
+            if s < NCH:
+                x_f = x_tiles[s][:].bitcast(F32)
+                grp[s] = gpool.tile([P, JC, K], BF16, name="grp", align_bytes=64)
+                g_f = grp[s][:].bitcast(F32)
+                late = []
+                for j in range(JC):
+                    xt = psum.tile([P, 4, P], F32, name="xt", tag="xt", bufs=6)
+                    for u in range(4):
+                        nc.tensor.transpose(xt[:, u, :], x_f[:, j, u * P:(u + 1) * P], ident_f[:])
+                    if (s * JC + j) in V_BANKS:
+                        late.append((j, xt))
+                    else:
+                        words_out(False, g_f[:, j, :], xt)
+            else:
+                late = []
+            q = s - 1
+            if 0 <= q < NCH:
+                codes[q] = cpool.tile([P, JC * K // 4], U32, name="codes", align_bytes=64)
+                scales[q] = cpool.tile([P, JC * K // 4], U8, name="scales", align_bytes=64)
+                nc.vector.quantize_mx(out=codes[q][:].bitcast(FP8X4), scales=scales[q][:],
+                                      in_=grp[q][:].rearrange("p j k -> p (j k)"))
+            for (j, xt) in late:
+                words_out(True, g_f[:, j, :], xt)
+            m = s - LAG
+            if 0 <= m < NCH:
+                acc = psum.tile([P, JC * O], F32, name="acc", tag="acc", bufs=2)
+                for j in range(JC):
+                    for g in range(2):
+                        c0 = (j * 2 + g) * P
+                        nc.tensor.matmul_mx(
+                            out=acc[:, j * O:(j + 1) * O],
+                            lhsT=codes[m][:, c0:c0 + P].bitcast(FP8X4),
+                            lhsT_scale=scales[m][:, c0:c0 + P],
+                            rhs=w_codes[:, g * O:(g + 1) * O].bitcast(FP8X4),
+                            rhs_scale=w_scales[:, g * O:(g + 1) * O],
+                            start=(g == 0), stop=(g == 1))
+                nc.vector.tensor_tensor(out=o_tiles[m][:], in0=acc[:], in1=o_tiles[m][:], op=ADD)
+                a, h = divmod(m, J // JC)
+                nc.sync.dma_start(out=out_v[a][:, h * JC * O:(h + 1) * JC * O], in_=o_tiles[m][:])

@@ -1,8 +1,6 @@
 from contextlib import ExitStack
 
-import concourse.bass as bass
 import concourse.mybir as mybir
-import concourse.tile as tile
 from concourse.masks import make_identity
 
 F32 = mybir.dt.float32
@@ -19,143 +17,178 @@ K = 1024
 O = 128
 R = 128
 J = 8
-JC = 4
-NCH = A * J // JC
 FLOPS = 2 * A * S * K * O + 2 * A * S * R * O
 
-MANUAL = True
-LAG = 2
+UNITS = [list(range(4 * c, 4 * c + 4)) for c in range(15)] + [[60, 61], [62, 63]]
+GROUPS = [[2 * i, 2 * i + 1] for i in range(7)] + [[14, 15, 16]]
+STORES = dict([(2 * i + 1, [2 * i, 2 * i + 1]) for i in range(7)] + [(14, [14]), (15, [15]), (16, [16])])
 V_BANKS = frozenset(range(3, 64, 8))
 
 
 def tile_linear_pa_t_kernel(tc, data, W, t_lora, lora_b, out):
     nc = tc.nc
     with ExitStack() as ctx:
-        if MANUAL:
-            ctx.enter_context(tc.manual_schedule())
+        ctx.enter_context(tc.manual_schedule())
         const = ctx.enter_context(tc.tile_pool(name="const", bufs=1))
-        xpool = ctx.enter_context(tc.tile_pool(name="xpool", bufs=10))
-        opool = ctx.enter_context(tc.tile_pool(name="opool", bufs=1))
+        xpool = ctx.enter_context(tc.tile_pool(name="xpool", bufs=5))
         ttp = ctx.enter_context(tc.tile_pool(name="ttp", bufs=3))
-        gpool = ctx.enter_context(tc.tile_pool(name="gpool", bufs=3))
-        cpool = ctx.enter_context(tc.tile_pool(name="cpool", bufs=3))
+        gpool = ctx.enter_context(tc.tile_pool(name="gpool", bufs=4))
+        cpool = ctx.enter_context(tc.tile_pool(name="cpool", bufs=4))
         psum = ctx.enter_context(tc.psum_pool(name="psum", bufs=1))
 
         data_v = data.rearrange("a (p j) k -> a p j k", j=J)
         t_v = t_lora.rearrange("a g (p j) r -> p (a g) (j r)", j=J)
         out_v = out.rearrange("a (p j) o -> a p (j o)", j=J)
-        lb_v = lora_b.rearrange("a o r -> o a r")
+        lb_v = lora_b.rearrange("a (h l) r -> (a h) (l r)", l=8)
 
-        ident_f = const.tile([P, P], F32, name="ident_f")
         ident_b = const.tile([P, P], BF16, name="ident_b")
+        ident_f = const.tile([P, P], F32, name="ident_f")
         make_identity(nc, ident_b[:])
         make_identity(nc, ident_f[:])
 
-        lb_sb = const.tile([P, A, R], BF16, name="lb_sb")
+        t_src = {}
+
+        def load_t(a0, n):
+            t_sb = const.tile([P, n, J * R], BF16, name="t_sb%d" % a0)
+            nc.sync.dma_start(out=t_sb[:], in_=t_v[:, a0:a0 + n, :])
+            for i in range(n):
+                t_src[a0 + i] = t_sb[:, i, :]
+
+        load_t(0, 1)
+        lb_sb = const.tile([P, 8 * R], BF16, name="lb_sb")
         nc.sync.dma_start(out=lb_sb[:], in_=lb_v)
-        t_a = const.tile([P, 2, J * R], BF16, name="t_a")
-        nc.sync.dma_start(out=t_a[:], in_=t_v[:, 0:2, :])
+        load_t(1, 1)
         w_sb = const.tile([P, K], BF16, name="w_sb")
         nc.sync.dma_start(out=w_sb[:], in_=W)
-        t_b = const.tile([P, A - 2, J * R], BF16, name="t_b")
-        nc.sync.dma_start(out=t_b[:], in_=t_v[:, 2:A, :])
-        x_tiles = []
-        for c in range(NCH):
-            x_sb = xpool.tile([P, JC, K], BF16, name="x_sb")
-            a, h = divmod(c, J // JC)
-            nc.sync.dma_start(out=x_sb[:], in_=data_v[a, :, h * JC:(h + 1) * JC, :])
-            x_tiles.append(x_sb)
+        load_t(2, 2)
+        load_t(4, 4)
+        x_words = {}
+        for a in range(A - 1):
+            x_sb = xpool.tile([P, J, K], BF16, name="x_sb")
+            nc.sync.dma_start(out=x_sb[:], in_=data_v[a])
+            for j in range(J):
+                x_words[a * J + j] = x_sb[:].bitcast(F32)[:, j, :]
+        for h in range(2):
+            x_half = xpool.tile([P, J // 2, K], BF16, name="x_half", bufs=2)
+            nc.sync.dma_start(out=x_half[:], in_=data_v[A - 1, :, h * 4:(h + 1) * 4, :])
+            for j in range(4):
+                x_words[(A - 1) * J + h * 4 + j] = x_half[:].bitcast(F32)[:, j, :]
 
-        o_tiles = [opool.tile([P, JC * O], F32, name="o_sb%d" % c) for c in range(NCH)]
+        o_sb = [const.tile([P, J * O], F32, name="o_sb%d" % a) for a in range(A)]
 
-        def words_out(eng_is_vector, dst_f32, bank):
+        def words_out(on_vector, dst_f32, bank):
             src = bank[:].rearrange("p (g u) t -> p g t u", u=2)
             dst = dst_f32.rearrange("p (g t u) -> p g t u", g=2, u=2)
-            if eng_is_vector:
+            if on_vector:
                 nc.vector.tensor_copy(out=dst, in_=src)
             else:
                 nc.scalar.copy(out=dst, in_=src)
 
         lbT = const.tile([P, A, O], BF16, name="lbT")
-        lbp = psum.tile([P, A, O], BF16, name="lbp", tag="acc", bufs=2)
-        for a in range(A):
-            nc.tensor.transpose(lbp[:, a, :], lb_sb[:, a, :], ident_b[:])
-        nc.vector.tensor_copy(out=lbT[:], in_=lbp[:])
-
         w_grp = const.tile([P, K], BF16, name="w_grp", align_bytes=64)
         w_codes = const.tile([P, K // 4], U32, name="w_codes", align_bytes=64)
         w_scales = const.tile([P, K // 4], U8, name="w_scales", align_bytes=64)
-
         tT = {}
-        for a in range(A + 1):
+
+        def lora_transposes(a):
+            tlp = psum.tile([P, J, P], BF16, name="tlp", tag="acc", bufs=2)
+            for j in range(J):
+                nc.tensor.transpose(tlp[:, j, :], t_src[a][:, j * R:(j + 1) * R], ident_b[:])
+            tT[a] = ttp.tile([P, J, P], BF16, name="tT")
+            nc.vector.tensor_copy(out=tT[a][:], in_=tlp[:])
+
+        def lora_b_transposes():
+            lbp = psum.tile([P, 8, P], BF16, name="lbp", tag="acc", bufs=2)
+            for l in range(8):
+                nc.tensor.transpose(lbp[:, l, :], lb_sb[:, l * R:(l + 1) * R], ident_b[:])
+            nc.vector.tensor_copy(out=lbT[:].rearrange("p a (h l) -> p a h l", l=8),
+                                  in_=lbp[:].rearrange("p l (a h) -> p a h l", a=A))
+
+        def lora_matmuls(a):
+            for h in range(2):
+                dl = psum.tile([P, 4 * O], F32, name="dl", tag="xt", bufs=6)
+                for j in range(4):
+                    nc.tensor.matmul(dl[:, j * O:(j + 1) * O], lhsT=tT[a][:, h * 4 + j, :],
+                                     rhs=lbT[:, a, :], start=True, stop=True)
+                dst = o_sb[a][:, h * 4 * O:(h + 1) * 4 * O]
+                if h == 1 and a % 2 == 0:
+                    nc.vector.tensor_scalar_mul(out=dst, in0=dl[:], scalar1=2.0)
+                else:
+                    nc.scalar.mul(out=dst, in_=dl[:], mul=2.0)
+
+        lora_transposes(0)
+        lora_b_transposes()
+        for a in range(1, A + 1):
             if a < A:
-                src = t_a[:, a, :] if a < 2 else t_b[:, a - 2, :]
-                tlp = psum.tile([P, J, P], BF16, name="tlp", tag="acc", bufs=2)
-                for j in range(J):
-                    nc.tensor.transpose(tlp[:, j, :], src[:, j * R:(j + 1) * R], ident_b[:])
-                tT[a] = ttp.tile([P, J, P], BF16, name="tT")
-                nc.vector.tensor_copy(out=tT[a][:], in_=tlp[:])
-            if a == 1:
+                lora_transposes(a)
+            if a == 2:
                 wp = psum.tile([P, 4, P], F32, name="wp", tag="xt", bufs=6)
-                w_f = w_sb[:].bitcast(F32)
                 for u in range(4):
-                    nc.tensor.transpose(wp[:, u, :], w_f[:, u * P:(u + 1) * P], ident_f[:])
+                    nc.tensor.transpose(wp[:, u, :], w_sb[:].bitcast(F32)[:, u * P:(u + 1) * P], ident_f[:])
                 words_out(False, w_grp[:].bitcast(F32), wp)
-            if a == 3:
+            if a == 4:
                 nc.vector.quantize_mx(out=w_codes[:].bitcast(FP8X4), scales=w_scales[:], in_=w_grp[:])
-            if a >= 1:
-                b = a - 1
-                for h in range(J // JC):
-                    dl = psum.tile([P, JC * O], F32, name="dl", tag="xt", bufs=6)
-                    for j in range(JC):
-                        nc.tensor.matmul(dl[:, j * O:(j + 1) * O], lhsT=tT[b][:, h * JC + j, :],
-                                         rhs=lbT[:, b, :], start=True, stop=True)
-                    dst = o_tiles[b * (J // JC) + h]
-                    if h == 1 and b % 2 == 0:
-                        nc.vector.tensor_scalar_mul(out=dst[:], in0=dl[:], scalar1=2.0)
-                    else:
-                        nc.scalar.mul(out=dst[:], in_=dl[:], mul=2.0)
+            lora_matmuls(a - 1)
 
         grp = {}
         codes = {}
         scales = {}
-        for s in range(NCH + LAG):
-            if s < NCH:
-                x_f = x_tiles[s][:].bitcast(F32)
-                grp[s] = gpool.tile([P, JC, K], BF16, name="grp", align_bytes=64)
-                g_f = grp[s][:].bitcast(F32)
-                late = []
-                for j in range(JC):
-                    xt = psum.tile([P, 4, P], F32, name="xt", tag="xt", bufs=6)
-                    for u in range(4):
-                        nc.tensor.transpose(xt[:, u, :], x_f[:, j, u * P:(u + 1) * P], ident_f[:])
-                    if (s * JC + j) in V_BANKS:
-                        late.append((j, xt))
-                    else:
-                        words_out(False, g_f[:, j, :], xt)
-            else:
-                late = []
-            q = s - 1
-            if 0 <= q < NCH:
-                codes[q] = cpool.tile([P, JC * K // 4], U32, name="codes", align_bytes=64)
-                scales[q] = cpool.tile([P, JC * K // 4], U8, name="scales", align_bytes=64)
-                nc.vector.quantize_mx(out=codes[q][:].bitcast(FP8X4), scales=scales[q][:],
-                                      in_=grp[q][:].rearrange("p j k -> p (j k)"))
-            for (j, xt) in late:
-                words_out(True, g_f[:, j, :], xt)
-            m = s - LAG
-            if 0 <= m < NCH:
-                acc = psum.tile([P, JC * O], F32, name="acc", tag="acc", bufs=2)
-                for j in range(JC):
-                    for g in range(2):
-                        c0 = (j * 2 + g) * P
-                        nc.tensor.matmul_mx(
-                            out=acc[:, j * O:(j + 1) * O],
-                            lhsT=codes[m][:, c0:c0 + P].bitcast(FP8X4),
-                            lhsT_scale=scales[m][:, c0:c0 + P],
-                            rhs=w_codes[:, g * O:(g + 1) * O].bitcast(FP8X4),
-                            rhs_scale=w_scales[:, g * O:(g + 1) * O],
-                            start=(g == 0), stop=(g == 1))
-                nc.vector.tensor_tensor(out=o_tiles[m][:], in0=acc[:], in1=o_tiles[m][:], op=ADD)
-                a, h = divmod(m, J // JC)
-                nc.sync.dma_start(out=out_v[a][:, h * JC * O:(h + 1) * JC * O], in_=o_tiles[m][:])
+        late = {}
+
+        def transposes(u):
+            grp[u] = gpool.tile([P, 4, K], BF16, name="grp", align_bytes=64)
+            late[u] = []
+            for i, t in enumerate(UNITS[u]):
+                xt = psum.tile([P, 4, P], F32, name="xt", tag="xt", bufs=6)
+                for q in range(4):
+                    nc.tensor.transpose(xt[:, q, :], x_words[t][:, q * P:(q + 1) * P], ident_f[:])
+                if t in V_BANKS:
+                    late[u].append((i, xt))
+                else:
+                    words_out(False, grp[u][:].bitcast(F32)[:, i, :], xt)
+
+        def vector_copies(u):
+            for (i, xt) in late[u]:
+                words_out(True, grp[u][:].bitcast(F32)[:, i, :], xt)
+
+        def quantise(u):
+            n = len(UNITS[u])
+            codes[u] = cpool.tile([P, K], U32, name="codes", align_bytes=64)
+            scales[u] = cpool.tile([P, K], U8, name="scales", align_bytes=64)
+            nc.vector.quantize_mx(out=codes[u][:, 0:n * K // 4].bitcast(FP8X4), scales=scales[u][:, 0:n * K // 4],
+                                  in_=grp[u][:, 0:n, :].rearrange("p j k -> p (j k)"))
+
+        def multiply_add_store(u):
+            n = len(UNITS[u])
+            acc = psum.tile([P, 4 * O], F32, name="acc", tag="acc", bufs=2)
+            for i in range(n):
+                for g in range(2):
+                    c0 = (i * 2 + g) * P
+                    nc.tensor.matmul_mx(
+                        out=acc[:, i * O:(i + 1) * O],
+                        lhsT=codes[u][:, c0:c0 + P].bitcast(FP8X4),
+                        lhsT_scale=scales[u][:, c0:c0 + P],
+                        rhs=w_codes[:, g * O:(g + 1) * O].bitcast(FP8X4),
+                        rhs_scale=w_scales[:, g * O:(g + 1) * O],
+                        start=(g == 0), stop=(g == 1))
+            a, j0 = divmod(UNITS[u][0], J)
+            dst = o_sb[a][:, j0 * O:(j0 + n) * O]
+            nc.vector.tensor_tensor(out=dst, in0=acc[:, 0:n * O], in1=dst, op=ADD)
+            if u in STORES:
+                first = UNITS[STORES[u][0]][0] % J
+                last = UNITS[STORES[u][-1]][-1] % J
+                nc.sync.dma_start(out=out_v[a][:, first * O:(last + 1) * O], in_=o_sb[a][:, first * O:(last + 1) * O])
+
+        for i in range(len(GROUPS) + 1):
+            now = GROUPS[i] if i < len(GROUPS) else []
+            before = GROUPS[i - 1] if i > 0 else []
+            for u in now:
+                transposes(u)
+            for u in before[-1:]:
+                quantise(u)
+            for u in now:
+                vector_copies(u)
+            for u in now[:-1]:
+                quantise(u)
+            for u in before:
+                multiply_add_store(u)

@@ -19,9 +19,9 @@ R = 128
 J = 8
 FLOPS = 2 * A * S * K * O + 2 * A * S * R * O
 
-UNITS = [list(range(4 * c, 4 * c + 4)) for c in range(15)] + [[60, 61], [62, 63]]
-GROUPS = [[2 * i, 2 * i + 1] for i in range(7)] + [[14, 15, 16]]
-STORES = dict([(2 * i + 1, [2 * i, 2 * i + 1]) for i in range(7)] + [(14, [14]), (15, [15]), (16, [16])])
+UNITS = [list(range(4 * c, 4 * c + 4)) for c in range(16)]
+GROUPS = [[u] for u in range(16)]
+STORES = dict([(u, [u]) for u in range(16)])
 V_BANKS = frozenset(range(3, 64, 8))
 
 
@@ -63,16 +63,12 @@ def tile_linear_pa_t_kernel(tc, data, W, t_lora, lora_b, out):
         load_t(2, 2)
         load_t(4, 4)
         x_words = {}
-        for a in range(A - 1):
-            x_sb = xpool.tile([P, J, K], BF16, name="x_sb")
-            nc.sync.dma_start(out=x_sb[:], in_=data_v[a])
-            for j in range(J):
-                x_words[a * J + j] = x_sb[:].bitcast(F32)[:, j, :]
-        for h in range(2):
-            x_half = xpool.tile([P, J // 2, K], BF16, name="x_half", bufs=2)
-            nc.sync.dma_start(out=x_half[:], in_=data_v[A - 1, :, h * 4:(h + 1) * 4, :])
+        for c in range(2 * A):
+            a, h = divmod(c, 2)
+            x_half = xpool.tile([P, J // 2, K], BF16, name="x_half", bufs=10)
+            nc.sync.dma_start(out=x_half[:], in_=data_v[a, :, h * 4:(h + 1) * 4, :])
             for j in range(4):
-                x_words[(A - 1) * J + h * 4 + j] = x_half[:].bitcast(F32)[:, j, :]
+                x_words[c * 4 + j] = x_half[:].bitcast(F32)[:, j, :]
 
         o_sb = [const.tile([P, J * O], F32, name="o_sb%d" % a) for a in range(A)]
 
@@ -179,16 +175,13 @@ def tile_linear_pa_t_kernel(tc, data, W, t_lora, lora_b, out):
                 last = UNITS[STORES[u][-1]][-1] % J
                 nc.sync.dma_start(out=out_v[a][:, first * O:(last + 1) * O], in_=o_sb[a][:, first * O:(last + 1) * O])
 
-        for i in range(len(GROUPS) + 1):
-            now = GROUPS[i] if i < len(GROUPS) else []
-            before = GROUPS[i - 1] if i > 0 else []
-            for u in now:
+        n_groups = len(GROUPS)
+        for i in range(n_groups + 2):
+            for u in (GROUPS[i] if i < n_groups else []):
                 transposes(u)
-            for u in before[-1:]:
+            for u in (GROUPS[i - 1] if 0 <= i - 1 < n_groups else []):
                 quantise(u)
-            for u in now:
+            for u in (GROUPS[i] if i < n_groups else []):
                 vector_copies(u)
-            for u in now[:-1]:
-                quantise(u)
-            for u in before:
+            for u in (GROUPS[i - 2] if 0 <= i - 2 < n_groups else []):
                 multiply_add_store(u)

@@ -21,7 +21,7 @@ FLOPS = 2 * A * S * K * O + 2 * A * S * R * O
 
 UNITS = [list(range(4 * c, 4 * c + 4)) for c in range(16)]
 GROUPS = [[u] for u in range(16)]
-STORES = dict([(u, [u]) for u in range(16)])
+STORES = dict([(2 * a + 1, [2 * a, 2 * a + 1]) for a in range(7)] + [(14, [14]), (15, [15])])
 V_BANKS = frozenset(range(3, 64, 8))
 
 
@@ -63,12 +63,18 @@ def tile_linear_pa_t_kernel(tc, data, W, t_lora, lora_b, out):
         load_t(2, 2)
         load_t(4, 4)
         x_words = {}
-        for c in range(2 * A):
-            a, h = divmod(c, 2)
-            x_half = xpool.tile([P, J // 2, K], BF16, name="x_half", bufs=10)
-            nc.sync.dma_start(out=x_half[:], in_=data_v[a, :, h * 4:(h + 1) * 4, :])
-            for j in range(4):
-                x_words[c * 4 + j] = x_half[:].bitcast(F32)[:, j, :]
+        for a in range(A):
+            if 0 < a < A - 1:
+                x_sb = xpool.tile([P, J, K], BF16, name="x_sb", bufs=4)
+                nc.sync.dma_start(out=x_sb[:], in_=data_v[a])
+                for j in range(J):
+                    x_words[a * J + j] = x_sb[:].bitcast(F32)[:, j, :]
+            else:
+                for h in range(2):
+                    x_half = xpool.tile([P, J // 2, K], BF16, name="x_half", bufs=4)
+                    nc.sync.dma_start(out=x_half[:], in_=data_v[a, :, h * 4:(h + 1) * 4, :])
+                    for j in range(4):
+                        x_words[a * J + h * 4 + j] = x_half[:].bitcast(F32)[:, j, :]
 
         o_sb = [const.tile([P, J * O], F32, name="o_sb%d" % a) for a in range(A)]
 

@@ -21,7 +21,8 @@ FLOPS = 2 * A * S * K * O + 2 * A * S * R * O
 
 UNITS = [list(range(4 * c, 4 * c + 4)) for c in range(16)]
 GROUPS = [[u] for u in range(16)]
-STORES = dict([(2 * a + 1, [2 * a, 2 * a + 1]) for a in range(7)] + [(14, [14]), (15, [15])])
+STORES = dict([(u, [u]) for u in range(16)])
+LATE_ADAPTER = 7
 V_BANKS = frozenset(range(3, 64, 8))
 
 
@@ -63,18 +64,12 @@ def tile_linear_pa_t_kernel(tc, data, W, t_lora, lora_b, out):
         load_t(2, 2)
         load_t(4, 4)
         x_words = {}
-        for a in range(A):
-            if 0 < a < A - 1:
-                x_sb = xpool.tile([P, J, K], BF16, name="x_sb", bufs=4)
-                nc.sync.dma_start(out=x_sb[:], in_=data_v[a])
-                for j in range(J):
-                    x_words[a * J + j] = x_sb[:].bitcast(F32)[:, j, :]
-            else:
-                for h in range(2):
-                    x_half = xpool.tile([P, J // 2, K], BF16, name="x_half", bufs=4)
-                    nc.sync.dma_start(out=x_half[:], in_=data_v[a, :, h * 4:(h + 1) * 4, :])
-                    for j in range(4):
-                        x_words[a * J + h * 4 + j] = x_half[:].bitcast(F32)[:, j, :]
+        for c in range(2 * A):
+            a, h = divmod(c, 2)
+            x_half = xpool.tile([P, J // 2, K], BF16, name="x_half", bufs=10)
+            nc.sync.dma_start(out=x_half[:], in_=data_v[a, :, h * 4:(h + 1) * 4, :])
+            for j in range(4):
+                x_words[c * 4 + j] = x_half[:].bitcast(F32)[:, j, :]
 
         o_sb = [const.tile([P, J * O], F32, name="o_sb%d" % a) for a in range(A)]
 
@@ -130,7 +125,8 @@ def tile_linear_pa_t_kernel(tc, data, W, t_lora, lora_b, out):
                 words_out(False, w_grp[:].bitcast(F32), wp)
             if a == 4:
                 nc.vector.quantize_mx(out=w_codes[:].bitcast(FP8X4), scales=w_scales[:], in_=w_grp[:])
-            lora_matmuls(a - 1)
+            if a - 1 != LATE_ADAPTER:
+                lora_matmuls(a - 1)
 
         grp = {}
         codes = {}
@@ -185,6 +181,8 @@ def tile_linear_pa_t_kernel(tc, data, W, t_lora, lora_b, out):
         for i in range(n_groups + 2):
             for u in (GROUPS[i] if i < n_groups else []):
                 transposes(u)
+            if i == n_groups - 1:
+                lora_matmuls(LATE_ADAPTER)
             for u in (GROUPS[i - 1] if 0 <= i - 1 < n_groups else []):
                 quantise(u)
             for u in (GROUPS[i] if i < n_groups else []):

@@ -19,9 +19,9 @@ R = 128
 J = 8
 FLOPS = 2 * A * S * K * O + 2 * A * S * R * O
 
-UNITS = [list(range(4 * c, 4 * c + 4)) for c in range(16)]
-GROUPS = [[u] for u in range(16)]
-STORES = dict([(u, [u]) for u in range(16)])
+UNITS = [list(range(4 * c, 4 * c + 4)) for c in range(15)] + [[60, 61], [62, 63]]
+GROUPS = [[u] for u in range(15)] + [[15, 16]]
+STORES = dict([(2 * a + 1, [2 * a, 2 * a + 1]) for a in range(6)] + [(u, [u]) for u in range(12, 17)])
 LATE_ADAPTER = 7
 V_BANKS = frozenset(range(3, 64, 8))
 

@@ -19,9 +19,9 @@ R = 128
 J = 8
 FLOPS = 2 * A * S * K * O + 2 * A * S * R * O
 
-UNITS = [list(range(4 * c, 4 * c + 4)) for c in range(15)] + [[60, 61], [62, 63]]
-GROUPS = [[u] for u in range(15)] + [[15, 16]]
-STORES = dict([(2 * a + 1, [2 * a, 2 * a + 1]) for a in range(6)] + [(u, [u]) for u in range(12, 17)])
+UNITS = [list(range(4 * c, 4 * c + 4)) for c in range(16)]
+GROUPS = [[u] for u in range(16)]
+STORES = dict([(u, [u]) for u in range(16)])
 LATE_ADAPTER = 7
 V_BANKS = frozenset(range(3, 64, 8))
 
@@ -29,7 +29,6 @@ V_BANKS = frozenset(range(3, 64, 8))
 def tile_linear_pa_t_kernel(tc, data, W, t_lora, lora_b, out):
     nc = tc.nc
     with ExitStack() as ctx:
-        ctx.enter_context(tc.manual_schedule())
         const = ctx.enter_context(tc.tile_pool(name="const", bufs=1))
         xpool = ctx.enter_context(tc.tile_pool(name="xpool", bufs=5))
         ttp = ctx.enter_context(tc.tile_pool(name="ttp", bufs=3))

@@ -29,6 +29,7 @@ V_BANKS = frozenset(range(3, 64, 8))
 def tile_linear_pa_t_kernel(tc, data, W, t_lora, lora_b, out):
     nc = tc.nc
     with ExitStack() as ctx:
+        ctx.enter_context(tc.manual_schedule())
         const = ctx.enter_context(tc.tile_pool(name="const", bufs=1))
         xpool = ctx.enter_context(tc.tile_pool(name="xpool", bufs=5))
         ttp = ctx.enter_context(tc.tile_pool(name="ttp", bufs=3))
@@ -41,6 +42,8 @@ def tile_linear_pa_t_kernel(tc, data, W, t_lora, lora_b, out):
         out_v = out.rearrange("a (p j) o -> a p (j o)", j=J)
         lb_v = lora_b.rearrange("a (h l) r -> (a h) (l r)", l=8)
 
+        warm = const.tile([P, 512], BF16, name="warm")
+        nc.vector.memset(warm[:].bitcast(mybir.dt.int32), 0)
         ident_b = const.tile([P, P], BF16, name="ident_b")
         ident_f = const.tile([P, P], F32, name="ident_f")
         make_identity(nc, ident_b[:])
@@ -112,8 +115,16 @@ def tile_linear_pa_t_kernel(tc, data, W, t_lora, lora_b, out):
                 else:
                     nc.scalar.mul(out=dst, in_=dl[:], mul=2.0)
 
+        def warm_up(n):
+            wps = psum.tile([P, 512], F32, name="wps", tag="xt", bufs=6)
+            for i in range(n):
+                nc.tensor.matmul(wps[:], lhsT=warm[:, 0:P], rhs=warm[:], start=True, stop=True)
+
+        warm_up(5)
         lora_transposes(0)
+        warm_up(1)
         lora_b_transposes()
+        warm_up(1)
         for a in range(1, A + 1):
             if a < A:
                 lora_transposes(a)

from contextlib import ExitStack

import concourse.mybir as mybir
from concourse.masks import make_identity

F32 = mybir.dt.float32
BF16 = mybir.dt.bfloat16
U32 = mybir.dt.uint32
U8 = mybir.dt.uint8
FP8X4 = mybir.dt.float8_e4m3fn_x4
ADD = mybir.AluOpType.add

P = 128
A = 8
S = 1024
K = 1024
O = 128
R = 128
J = 8
FLOPS = 2 * A * S * K * O + 2 * A * S * R * O

UNITS = [list(range(4 * c, 4 * c + 4)) for c in range(16)]
GROUPS = [[u] for u in range(16)]
STORES = dict([(u, [u]) for u in range(16)])
LATE_ADAPTER = 7
V_BANKS = frozenset(range(3, 64, 8))


def tile_linear_pa_t_kernel(tc, data, W, t_lora, lora_b, out):
    nc = tc.nc
    with ExitStack() as ctx:
        ctx.enter_context(tc.manual_schedule())
        const = ctx.enter_context(tc.tile_pool(name="const", bufs=1))
        xpool = ctx.enter_context(tc.tile_pool(name="xpool", bufs=5))
        ttp = ctx.enter_context(tc.tile_pool(name="ttp", bufs=3))
        gpool = ctx.enter_context(tc.tile_pool(name="gpool", bufs=4))
        cpool = ctx.enter_context(tc.tile_pool(name="cpool", bufs=4))
        psum = ctx.enter_context(tc.psum_pool(name="psum", bufs=1))

        data_v = data.rearrange("a (p j) k -> a p j k", j=J)
        t_v = t_lora.rearrange("a g (p j) r -> p (a g) (j r)", j=J)
        out_v = out.rearrange("a (p j) o -> a p (j o)", j=J)
        lb_v = lora_b.rearrange("a (h l) r -> (a h) (l r)", l=8)

        warm = const.tile([P, 512], BF16, name="warm")
        nc.vector.memset(warm[:].bitcast(mybir.dt.int32), 0)
        ident_b = const.tile([P, P], BF16, name="ident_b")
        ident_f = const.tile([P, P], F32, name="ident_f")
        make_identity(nc, ident_b[:])
        make_identity(nc, ident_f[:])

        t_src = {}

        def load_t(a0, n):
            t_sb = const.tile([P, n, J * R], BF16, name="t_sb%d" % a0)
            nc.sync.dma_start(out=t_sb[:], in_=t_v[:, a0:a0 + n, :])
            for i in range(n):
                t_src[a0 + i] = t_sb[:, i, :]

        load_t(0, 1)
        lb_sb = const.tile([P, 8 * R], BF16, name="lb_sb")
        nc.sync.dma_start(out=lb_sb[:], in_=lb_v)
        load_t(1, 1)
        w_sb = const.tile([P, K], BF16, name="w_sb")
        nc.sync.dma_start(out=w_sb[:], in_=W)
        load_t(2, 2)
        load_t(4, 4)
        x_words = {}
        for c in range(2 * A):
            a, h = divmod(c, 2)
            x_half = xpool.tile([P, J // 2, K], BF16, name="x_half", bufs=10)
            nc.sync.dma_start(out=x_half[:], in_=data_v[a, :, h * 4:(h + 1) * 4, :])
            for j in range(4):
                x_words[c * 4 + j] = x_half[:].bitcast(F32)[:, j, :]

        o_sb = [const.tile([P, J * O], F32, name="o_sb%d" % a) for a in range(A)]

        def words_out(on_vector, dst_f32, bank):
            src = bank[:].rearrange("p (g u) t -> p g t u", u=2)
            dst = dst_f32.rearrange("p (g t u) -> p g t u", g=2, u=2)
            if on_vector:
                nc.vector.tensor_copy(out=dst, in_=src)
            else:
                nc.scalar.copy(out=dst, in_=src)

        lbT = const.tile([P, A, O], BF16, name="lbT")
        w_grp = const.tile([P, K], BF16, name="w_grp", align_bytes=64)
        w_codes = const.tile([P, K // 4], U32, name="w_codes", align_bytes=64)
        w_scales = const.tile([P, K // 4], U8, name="w_scales", align_bytes=64)
        tT = {}

        def lora_transposes(a):
            tlp = psum.tile([P, J, P], BF16, name="tlp", tag="acc", bufs=2)
            for j in range(J):
                nc.tensor.transpose(tlp[:, j, :], t_src[a][:, j * R:(j + 1) * R], ident_b[:])
            tT[a] = ttp.tile([P, J, P], BF16, name="tT")
            nc.vector.tensor_copy(out=tT[a][:], in_=tlp[:])

        def lora_b_transposes():
            lbp = psum.tile([P, 8, P], BF16, name="lbp", tag="acc", bufs=2)
            for l in range(8):
                nc.tensor.transpose(lbp[:, l, :], lb_sb[:, l * R:(l + 1) * R], ident_b[:])
            nc.vector.tensor_copy(out=lbT[:].rearrange("p a (h l) -> p a h l", l=8),
                                  in_=lbp[:].rearrange("p l (a h) -> p a h l", a=A))

        def lora_matmuls(a):
            for h in range(2):
                dl = psum.tile([P, 4 * O], F32, name="dl", tag="xt", bufs=6)
                for j in range(4):
                    nc.tensor.matmul(dl[:, j * O:(j + 1) * O], lhsT=tT[a][:, h * 4 + j, :],
                                     rhs=lbT[:, a, :], start=True, stop=True)
                dst = o_sb[a][:, h * 4 * O:(h + 1) * 4 * O]
                if h == 1 and a % 2 == 0:
                    nc.vector.tensor_scalar_mul(out=dst, in0=dl[:], scalar1=2.0)
                else:
                    nc.scalar.mul(out=dst, in_=dl[:], mul=2.0)

        def warm_up(n):
            wps = psum.tile([P, 512], F32, name="wps", tag="xt", bufs=6)
            for i in range(n):
                nc.tensor.matmul(wps[:], lhsT=warm[:, 0:P], rhs=warm[:], start=True, stop=True)

        warm_up(5)
        lora_transposes(0)
        warm_up(1)
        lora_b_transposes()
        warm_up(1)
        for a in range(1, A + 1):
            if a < A:
                lora_transposes(a)
            if a == 2:
                wp = psum.tile([P, 4, P], F32, name="wp", tag="xt", bufs=6)
                for u in range(4):
                    nc.tensor.transpose(wp[:, u, :], w_sb[:].bitcast(F32)[:, u * P:(u + 1) * P], ident_f[:])
                words_out(False, w_grp[:].bitcast(F32), wp)
            if a == 4:
                nc.vector.quantize_mx(out=w_codes[:].bitcast(FP8X4), scales=w_scales[:], in_=w_grp[:])
            if a - 1 != LATE_ADAPTER:
                lora_matmuls(a - 1)

        grp = {}
        codes = {}
        scales = {}
        late = {}

        def transposes(u):
            grp[u] = gpool.tile([P, 4, K], BF16, name="grp", align_bytes=64)
            late[u] = []
            for i, t in enumerate(UNITS[u]):
                xt = psum.tile([P, 4, P], F32, name="xt", tag="xt", bufs=6)
                for q in range(4):
                    nc.tensor.transpose(xt[:, q, :], x_words[t][:, q * P:(q + 1) * P], ident_f[:])
                if t in V_BANKS:
                    late[u].append((i, xt))
                else:
                    words_out(False, grp[u][:].bitcast(F32)[:, i, :], xt)

        def vector_copies(u):
            for (i, xt) in late[u]:
                words_out(True, grp[u][:].bitcast(F32)[:, i, :], xt)

        def quantise(u):
            n = len(UNITS[u])
            codes[u] = cpool.tile([P, K], U32, name="codes", align_bytes=64)
            scales[u] = cpool.tile([P, K], U8, name="scales", align_bytes=64)
            nc.vector.quantize_mx(out=codes[u][:, 0:n * K // 4].bitcast(FP8X4), scales=scales[u][:, 0:n * K // 4],
                                  in_=grp[u][:, 0:n, :].rearrange("p j k -> p (j k)"))

        def multiply_add_store(u):
            n = len(UNITS[u])
            acc = psum.tile([P, 4 * O], F32, name="acc", tag="acc", bufs=2)
            for i in range(n):
                for g in range(2):
                    c0 = (i * 2 + g) * P
                    nc.tensor.matmul_mx(
                        out=acc[:, i * O:(i + 1) * O],
                        lhsT=codes[u][:, c0:c0 + P].bitcast(FP8X4),
                        lhsT_scale=scales[u][:, c0:c0 + P],
                        rhs=w_codes[:, g * O:(g + 1) * O].bitcast(FP8X4),
                        rhs_scale=w_scales[:, g * O:(g + 1) * O],
                        start=(g == 0), stop=(g == 1))
            a, j0 = divmod(UNITS[u][0], J)
            dst = o_sb[a][:, j0 * O:(j0 + n) * O]
            nc.vector.tensor_tensor(out=dst, in0=acc[:, 0:n * O], in1=dst, op=ADD)
            if u in STORES:
                first = UNITS[STORES[u][0]][0] % J
                last = UNITS[STORES[u][-1]][-1] % J
                nc.sync.dma_start(out=out_v[a][:, first * O:(last + 1) * O], in_=o_sb[a][:, first * O:(last + 1) * O])

        n_groups = len(GROUPS)
        for i in range(n_groups + 2):
            for u in (GROUPS[i] if i < n_groups else []):
                transposes(u)
            if i == n_groups - 1:
                lora_matmuls(LATE_ADAPTER)
            for u in (GROUPS[i - 1] if 0 <= i - 1 < n_groups else []):
                quantise(u)
            for u in (GROUPS[i] if i < n_groups else []):
                vector_copies(u)
            for u in (GROUPS[i - 2] if 0 <= i - 2 < n_groups else []):
                multiply_add_store(u)
